import numpy as np
import ml_dtypes

BF16 = ml_dtypes.bfloat16


def bf(x):
    return np.asarray(x, np.float32).astype(BF16)


def f32(x):
    return np.asarray(x, np.float32)


def f64(x):
    return np.asarray(x).astype(np.float64)


def striped(idx):
    return np.tile(idx.reshape(-1, 16).T, (8, 1))


V, D, M, N = 2048, 128, 256, 1024
EPS = 1e-5


def setup_inputs():
    return {"table": bf(np.random.standard_normal((V, D))), "att_scale": f32(1.0 + 0.1 * np.random.standard_normal((D, 1))), "w": bf(np.random.standard_normal((D, M)) / np.sqrt(D)), "b": f32(0.1 * np.random.standard_normal((M, 1))), "offs": striped(np.random.permutation(np.tile(np.arange(V), 2))[:N])}


def reference(table, att_scale, w, b, offs):
    idx = offs[:16].T.reshape(-1)
    t = f64(table)
    hn = f64(att_scale)[:, 0][None, :] * t / np.sqrt(np.mean(t * t, axis=1, keepdims=True) + EPS)
    return f64(w).T @ hn[idx].T + f64(b)

@@ -1,0 +1,81 @@
+import concourse.mybir as mybir
+from concourse.masks import make_identity
+
+BF16, F32, U16 = mybir.dt.bfloat16, mybir.dt.float32, mybir.dt.uint16
+ACT = mybir.ActivationFunctionType
+
+P = 128
+V, D, M, N = 2048, 128, 256, 1024
+EPS = 1e-5
+BLOCKS_PER_CHUNK = 4
+CHUNK = BLOCKS_PER_CHUNK * P
+CHUNKS = V // CHUNK
+PIECE = 512
+FLOPS = 2 * D * M * N
+
+
+def tile_gqa_kernel(tc, table, att_scale, w, b, offs, out):
+    nc = tc.nc
+    table_chunks = table.rearrange("(c k p) d -> c p k d", k=BLOCKS_PER_CHUNK, p=P)
+
+    with (
+        tc.tile_pool(name="held", bufs=1) as held,
+        tc.tile_pool(name="work", bufs=2) as work,
+        tc.psum_pool(name="flip", bufs=CHUNKS) as flip,
+        tc.psum_pool(name="prod", bufs=4) as prod,
+    ):
+        rows = [held.tile([P, BLOCKS_PER_CHUNK, D], BF16, name=f"rows{c}") for c in range(CHUNKS)]
+        for c in range(CHUNKS):
+            queue = nc.sync if c % 2 == 0 else nc.scalar
+            queue.dma_start(rows[c][:], table_chunks[c])
+        offsets = held.tile([P, N // 16], U16, name="offsets")
+        nc.sync.dma_start(offsets[:], offs)
+        gain = held.tile([D, 1], F32, name="gain")
+        nc.sync.dma_start(gain[:], att_scale)
+        weights = held.tile([D, M], BF16, name="weights")
+        nc.scalar.dma_start(weights[:], w)
+        bias = [held.tile([P, 1], F32, name=f"bias{h}") for h in range(M // P)]
+        for h in range(M // P):
+            nc.gpsimd.dma_start(bias[h][:], b[h * P : (h + 1) * P, :])
+
+        identity = held.tile([P, P], F32, name="identity")
+        make_identity(nc, identity[:])
+        eps = held.tile([P, 1], F32, name="eps")
+        nc.vector.memset(eps[:], EPS)
+        first = held.tile([P, 1], F32, name="first")
+        nc.scalar.activation(first[:], eps[:], ACT.Sqrt)
+
+        normed = held.tile([D, V], BF16, name="normed")
+        for c in range(CHUNKS):
+            sumsq = work.tile([P, BLOCKS_PER_CHUNK], F32, name="sumsq")
+            for k in range(BLOCKS_PER_CHUNK):
+                squares = work.tile([P, D], BF16, name="squares")
+                nc.scalar.activation(
+                    squares[:], rows[c][:, k, :], ACT.Square, accum_out=sumsq[:, k : k + 1]
+                )
+            rms = work.tile([P, BLOCKS_PER_CHUNK], F32, name="rms")
+            nc.scalar.activation(rms[:], sumsq[:], ACT.Sqrt, bias=eps[:], scale=1.0 / D)
+            rstd = work.tile([P, BLOCKS_PER_CHUNK], F32, name="rstd")
+            nc.vector.reciprocal(rstd[:], rms[:])
+            scaled = work.tile([P, BLOCKS_PER_CHUNK, D], F32, name="scaled")
+            for k in range(BLOCKS_PER_CHUNK):
+                nc.vector.tensor_scalar_mul(scaled[:, k, :], rows[c][:, k, :], rstd[:, k : k + 1])
+            flipped = flip.tile([D, CHUNK], F32, name="flipped")
+            for k in range(BLOCKS_PER_CHUNK):
+                nc.tensor.transpose(flipped[:, k * P : (k + 1) * P], scaled[:, k, :], identity[:])
+            nc.vector.tensor_scalar_mul(normed[:, c * CHUNK : (c + 1) * CHUNK], flipped[:], gain[:])
+
+        for j in range(N // PIECE):
+            looked_up = normed[:].indirect(offsets[:, j * (PIECE // 16) : (j + 1) * (PIECE // 16)])
+            for h in range(M // P):
+                product = prod.tile([P, PIECE], F32, name="product")
+                nc.tensor.matmul(
+                    product[:], weights[:, h * P : (h + 1) * P], looked_up, start=True, stop=True
+                )
+                biased = work.tile([P, PIECE], F32, name="biased")
+                if h == 0:
+                    nc.scalar.activation(biased[:], product[:], ACT.Identity, bias=bias[h][:])
+                    nc.scalar.dma_start(out[h * P : (h + 1) * P, j * PIECE : (j + 1) * PIECE], biased[:])
+                else:
+                    nc.vector.tensor_scalar_add(biased[:], product[:], bias[h][:])
+                    nc.sync.dma_start(out[h * P : (h + 1) * P, j * PIECE : (j + 1) * PIECE], biased[:])

@@ -21,6 +21,7 @@ def tile_gqa_kernel(tc, table, att_scale, w, b, offs, out):
     with (
         tc.tile_pool(name="held", bufs=1) as held,
         tc.tile_pool(name="work", bufs=2) as work,
+        tc.tile_pool(name="done", bufs=4) as done,
         tc.psum_pool(name="flip", bufs=CHUNKS) as flip,
         tc.psum_pool(name="prod", bufs=4) as prod,
     ):
@@ -36,7 +37,7 @@ def tile_gqa_kernel(tc, table, att_scale, w, b, offs, out):
         nc.scalar.dma_start(weights[:], w)
         bias = [held.tile([P, 1], F32, name=f"bias{h}") for h in range(M // P)]
         for h in range(M // P):
-            nc.gpsimd.dma_start(bias[h][:], b[h * P : (h + 1) * P, :])
+            nc.sync.dma_start(bias[h][:], b[h * P : (h + 1) * P, :])
 
         identity = held.tile([P, P], F32, name="identity")
         make_identity(nc, identity[:])
@@ -72,7 +73,7 @@ def tile_gqa_kernel(tc, table, att_scale, w, b, offs, out):
                 nc.tensor.matmul(
                     product[:], weights[:, h * P : (h + 1) * P], looked_up, start=True, stop=True
                 )
-                biased = work.tile([P, PIECE], F32, name="biased")
+                biased = done.tile([P, PIECE], F32, name="biased")
                 if h == 0:
                     nc.scalar.activation(biased[:], product[:], ACT.Identity, bias=bias[h][:])
                     nc.scalar.dma_start(out[h * P : (h + 1) * P, j * PIECE : (j + 1) * PIECE], biased[:])

@@ -11,6 +11,7 @@ BLOCKS_PER_CHUNK = 4
 CHUNK = BLOCKS_PER_CHUNK * P
 CHUNKS = V // CHUNK
 PIECE = 512
+WARM_UP = 8
 FLOPS = 2 * D * M * N
 
 
@@ -22,8 +23,9 @@ def tile_gqa_kernel(tc, table, att_scale, w, b, offs, out):
         tc.tile_pool(name="held", bufs=1) as held,
         tc.tile_pool(name="work", bufs=2) as work,
         tc.tile_pool(name="done", bufs=4) as done,
-        tc.psum_pool(name="flip", bufs=CHUNKS) as flip,
+        tc.psum_pool(name="flip", bufs=3) as flip,
         tc.psum_pool(name="prod", bufs=4) as prod,
+        tc.psum_pool(name="idle", bufs=1) as idle,
     ):
         rows = [held.tile([P, BLOCKS_PER_CHUNK, D], BF16, name=f"rows{c}") for c in range(CHUNKS)]
         for c in range(CHUNKS):
@@ -46,6 +48,12 @@ def tile_gqa_kernel(tc, table, att_scale, w, b, offs, out):
         first = held.tile([P, 1], F32, name="first")
         nc.scalar.activation(first[:], eps[:], ACT.Sqrt)
 
+        zeros = held.tile([P, PIECE], BF16, name="zeros")
+        nc.vector.memset(zeros[:], 0.0)
+        unread = idle.tile([P, PIECE], F32, name="unread")
+        for i in range(WARM_UP):
+            nc.tensor.matmul(unread[:], zeros[:, 0:P], zeros[:], start=True, stop=True)
+
         normed = held.tile([D, V], BF16, name="normed")
         for c in range(CHUNKS):
             sumsq = work.tile([P, BLOCKS_PER_CHUNK], F32, name="sumsq")
@@ -65,6 +73,15 @@ def tile_gqa_kernel(tc, table, att_scale, w, b, offs, out):
             for k in range(BLOCKS_PER_CHUNK):
                 nc.tensor.transpose(flipped[:, k * P : (k + 1) * P], scaled[:, k, :], identity[:])
             nc.vector.tensor_scalar_mul(normed[:, c * CHUNK : (c + 1) * CHUNK], flipped[:], gain[:])
+            if c < CHUNKS - 1:
+                for h in range(M // P):
+                    nc.tensor.matmul(
+                        unread[:],
+                        weights[:, h * P : (h + 1) * P],
+                        normed[:, c * CHUNK : (c + 1) * CHUNK],
+                        start=True,
+                        stop=True,
+                    )
 
         for j in range(N // PIECE):
             looked_up = normed[:].indirect(offsets[:, j * (PIECE // 16) : (j + 1) * (PIECE // 16)])

@@ -3,6 +3,7 @@ from concourse.masks import make_identity
 
 BF16, F32, U16 = mybir.dt.bfloat16, mybir.dt.float32, mybir.dt.uint16
 ACT = mybir.ActivationFunctionType
+MULT = mybir.AluOpType.mult
 
 P = 128
 V, D, M, N = 2048, 128, 256, 1024
@@ -11,7 +12,6 @@ BLOCKS_PER_CHUNK = 4
 CHUNK = BLOCKS_PER_CHUNK * P
 CHUNKS = V // CHUNK
 PIECE = 512
-WARM_UP = 8
 FLOPS = 2 * D * M * N
 
 
@@ -23,38 +23,31 @@ def tile_gqa_kernel(tc, table, att_scale, w, b, offs, out):
         tc.tile_pool(name="held", bufs=1) as held,
         tc.tile_pool(name="work", bufs=2) as work,
         tc.tile_pool(name="done", bufs=4) as done,
-        tc.psum_pool(name="flip", bufs=3) as flip,
+        tc.psum_pool(name="flip", bufs=CHUNKS) as flip,
         tc.psum_pool(name="prod", bufs=4) as prod,
-        tc.psum_pool(name="idle", bufs=1) as idle,
     ):
         rows = [held.tile([P, BLOCKS_PER_CHUNK, D], BF16, name=f"rows{c}") for c in range(CHUNKS)]
         for c in range(CHUNKS):
             queue = nc.sync if c % 2 == 0 else nc.scalar
             queue.dma_start(rows[c][:], table_chunks[c])
+        gain = held.tile([P, D], F32, name="gain")
+        nc.sync.dma_start(gain[:], att_scale.rearrange("d one -> (d one)").partition_broadcast(P))
         offsets = held.tile([P, N // 16], U16, name="offsets")
         nc.sync.dma_start(offsets[:], offs)
-        gain = held.tile([D, 1], F32, name="gain")
-        nc.sync.dma_start(gain[:], att_scale)
         weights = held.tile([D, M], BF16, name="weights")
         nc.scalar.dma_start(weights[:], w)
         bias = [held.tile([P, 1], F32, name=f"bias{h}") for h in range(M // P)]
         for h in range(M // P):
             nc.sync.dma_start(bias[h][:], b[h * P : (h + 1) * P, :])
 
-        identity = held.tile([P, P], F32, name="identity")
+        identity = held.tile([P, P], BF16, name="identity")
         make_identity(nc, identity[:])
         eps = held.tile([P, 1], F32, name="eps")
         nc.vector.memset(eps[:], EPS)
         first = held.tile([P, 1], F32, name="first")
         nc.scalar.activation(first[:], eps[:], ACT.Sqrt)
 
-        zeros = held.tile([P, PIECE], BF16, name="zeros")
-        nc.vector.memset(zeros[:], 0.0)
-        unread = idle.tile([P, PIECE], F32, name="unread")
-        for i in range(WARM_UP):
-            nc.tensor.matmul(unread[:], zeros[:, 0:P], zeros[:], start=True, stop=True)
-
-        normed = held.tile([D, V], BF16, name="normed")
+        rstd = [held.tile([P, BLOCKS_PER_CHUNK], F32, name=f"rstd{c}") for c in range(CHUNKS)]
         for c in range(CHUNKS):
             sumsq = work.tile([P, BLOCKS_PER_CHUNK], F32, name="sumsq")
             for k in range(BLOCKS_PER_CHUNK):
@@ -64,24 +57,21 @@ def tile_gqa_kernel(tc, table, att_scale, w, b, offs, out):
                 )
             rms = work.tile([P, BLOCKS_PER_CHUNK], F32, name="rms")
             nc.scalar.activation(rms[:], sumsq[:], ACT.Sqrt, bias=eps[:], scale=1.0 / D)
-            rstd = work.tile([P, BLOCKS_PER_CHUNK], F32, name="rstd")
-            nc.vector.reciprocal(rstd[:], rms[:])
-            scaled = work.tile([P, BLOCKS_PER_CHUNK, D], F32, name="scaled")
+            nc.vector.reciprocal(rstd[c][:], rms[:])
+
+        normed = held.tile([D, V], BF16, name="normed")
+        for c in range(CHUNKS):
+            normed_rows = work.tile([P, BLOCKS_PER_CHUNK, D], BF16, name="normed_rows")
+            flipped = flip.tile([D, CHUNK], BF16, name="flipped")
             for k in range(BLOCKS_PER_CHUNK):
-                nc.vector.tensor_scalar_mul(scaled[:, k, :], rows[c][:, k, :], rstd[:, k : k + 1])
-            flipped = flip.tile([D, CHUNK], F32, name="flipped")
-            for k in range(BLOCKS_PER_CHUNK):
-                nc.tensor.transpose(flipped[:, k * P : (k + 1) * P], scaled[:, k, :], identity[:])
-            nc.vector.tensor_scalar_mul(normed[:, c * CHUNK : (c + 1) * CHUNK], flipped[:], gain[:])
+                nc.vector.scalar_tensor_tensor(
+                    normed_rows[:, k, :], rows[c][:, k, :], rstd[c][:, k : k + 1], gain[:], MULT, MULT
+                )
+                nc.tensor.transpose(flipped[:, k * P : (k + 1) * P], normed_rows[:, k, :], identity[:])
             if c < CHUNKS - 1:
-                for h in range(M // P):
-                    nc.tensor.matmul(
-                        unread[:],
-                        weights[:, h * P : (h + 1) * P],
-                        normed[:, c * CHUNK : (c + 1) * CHUNK],
-                        start=True,
-                        stop=True,
-                    )
+                nc.scalar.copy(normed[:, c * CHUNK : (c + 1) * CHUNK], flipped[:])
+            else:
+                nc.vector.tensor_copy(normed[:, c * CHUNK : (c + 1) * CHUNK], flipped[:])
 
         for j in range(N // PIECE):
             looked_up = normed[:].indirect(offsets[:, j * (PIECE // 16) : (j + 1) * (PIECE // 16)])

@@ -3,7 +3,6 @@ from concourse.masks import make_identity
 
 BF16, F32, U16 = mybir.dt.bfloat16, mybir.dt.float32, mybir.dt.uint16
 ACT = mybir.ActivationFunctionType
-MULT = mybir.AluOpType.mult
 
 P = 128
 V, D, M, N = 2048, 128, 256, 1024
@@ -17,7 +16,7 @@ FLOPS = 2 * D * M * N
 
 def tile_gqa_kernel(tc, table, att_scale, w, b, offs, out):
     nc = tc.nc
-    table_chunks = table.rearrange("(c k p) d -> c p k d", k=BLOCKS_PER_CHUNK, p=P)
+    table_chunks = table.rearrange("(c p k) d -> c p k d", k=BLOCKS_PER_CHUNK, p=P)
 
     with (
         tc.tile_pool(name="held", bufs=1) as held,
@@ -28,26 +27,25 @@ def tile_gqa_kernel(tc, table, att_scale, w, b, offs, out):
     ):
         rows = [held.tile([P, BLOCKS_PER_CHUNK, D], BF16, name=f"rows{c}") for c in range(CHUNKS)]
         for c in range(CHUNKS):
-            queue = nc.sync if c % 2 == 0 else nc.scalar
-            queue.dma_start(rows[c][:], table_chunks[c])
-        gain = held.tile([P, D], F32, name="gain")
-        nc.sync.dma_start(gain[:], att_scale.rearrange("d one -> (d one)").partition_broadcast(P))
+            nc.sync.dma_start(rows[c][:], table_chunks[c])
         offsets = held.tile([P, N // 16], U16, name="offsets")
         nc.sync.dma_start(offsets[:], offs)
+        gain = held.tile([D, 1], F32, name="gain")
+        nc.scalar.dma_start(gain[:], att_scale)
         weights = held.tile([D, M], BF16, name="weights")
         nc.scalar.dma_start(weights[:], w)
         bias = [held.tile([P, 1], F32, name=f"bias{h}") for h in range(M // P)]
         for h in range(M // P):
-            nc.sync.dma_start(bias[h][:], b[h * P : (h + 1) * P, :])
+            nc.scalar.dma_start(bias[h][:], b[h * P : (h + 1) * P, :])
 
-        identity = held.tile([P, P], BF16, name="identity")
+        identity = held.tile([P, P], F32, name="identity")
         make_identity(nc, identity[:])
         eps = held.tile([P, 1], F32, name="eps")
         nc.vector.memset(eps[:], EPS)
         first = held.tile([P, 1], F32, name="first")
         nc.scalar.activation(first[:], eps[:], ACT.Sqrt)
 
-        rstd = [held.tile([P, BLOCKS_PER_CHUNK], F32, name=f"rstd{c}") for c in range(CHUNKS)]
+        normed = held.tile([D, V], BF16, name="normed")
         for c in range(CHUNKS):
             sumsq = work.tile([P, BLOCKS_PER_CHUNK], F32, name="sumsq")
             for k in range(BLOCKS_PER_CHUNK):
@@ -57,21 +55,19 @@ def tile_gqa_kernel(tc, table, att_scale, w, b, offs, out):
                 )
             rms = work.tile([P, BLOCKS_PER_CHUNK], F32, name="rms")
             nc.scalar.activation(rms[:], sumsq[:], ACT.Sqrt, bias=eps[:], scale=1.0 / D)
-            nc.vector.reciprocal(rstd[c][:], rms[:])
-
-        normed = held.tile([D, V], BF16, name="normed")
-        for c in range(CHUNKS):
-            normed_rows = work.tile([P, BLOCKS_PER_CHUNK, D], BF16, name="normed_rows")
-            flipped = flip.tile([D, CHUNK], BF16, name="flipped")
+            rstd = work.tile([P, BLOCKS_PER_CHUNK], F32, name="rstd")
+            nc.vector.reciprocal(rstd[:], rms[:])
+            scaled = work.tile([P, BLOCKS_PER_CHUNK, D], F32, name="scaled")
             for k in range(BLOCKS_PER_CHUNK):
-                nc.vector.scalar_tensor_tensor(
-                    normed_rows[:, k, :], rows[c][:, k, :], rstd[c][:, k : k + 1], gain[:], MULT, MULT
-                )
-                nc.tensor.transpose(flipped[:, k * P : (k + 1) * P], normed_rows[:, k, :], identity[:])
-            if c < CHUNKS - 1:
-                nc.scalar.copy(normed[:, c * CHUNK : (c + 1) * CHUNK], flipped[:])
-            else:
-                nc.vector.tensor_copy(normed[:, c * CHUNK : (c + 1) * CHUNK], flipped[:])
+                nc.vector.tensor_scalar_mul(scaled[:, k, :], rows[c][:, k, :], rstd[:, k : k + 1])
+            flipped = flip.tile([D, CHUNK], F32, name="flipped")
+            for k in range(BLOCKS_PER_CHUNK):
+                nc.tensor.transpose(flipped[:, k * P : (k + 1) * P], scaled[:, k, :], identity[:])
+            nc.vector.tensor_scalar_mul(
+                normed[:, c * CHUNK : (c + 1) * CHUNK].rearrange("d (p k) -> d p k", k=BLOCKS_PER_CHUNK),
+                flipped[:].rearrange("d (k p) -> d p k", k=BLOCKS_PER_CHUNK),
+                gain[:],
+            )
 
         for j in range(N // PIECE):
             looked_up = normed[:].indirect(offsets[:, j * (PIECE // 16) : (j + 1) * (PIECE // 16)])

@@ -3,6 +3,7 @@ from concourse.masks import make_identity
 
 BF16, F32, U16 = mybir.dt.bfloat16, mybir.dt.float32, mybir.dt.uint16
 ACT = mybir.ActivationFunctionType
+MULT = mybir.AluOpType.mult
 
 P = 128
 V, D, M, N = 2048, 128, 256, 1024
@@ -10,42 +11,44 @@ EPS = 1e-5
 BLOCKS_PER_CHUNK = 4
 CHUNK = BLOCKS_PER_CHUNK * P
 CHUNKS = V // CHUNK
-PIECE = 512
+PIECE = 256
+PIECES = N // PIECE
+HALVES = M // P
 FLOPS = 2 * D * M * N
 
 
 def tile_gqa_kernel(tc, table, att_scale, w, b, offs, out):
     nc = tc.nc
-    table_chunks = table.rearrange("(c p k) d -> c p k d", k=BLOCKS_PER_CHUNK, p=P)
 
     with (
         tc.tile_pool(name="held", bufs=1) as held,
         tc.tile_pool(name="work", bufs=2) as work,
-        tc.tile_pool(name="done", bufs=4) as done,
-        tc.psum_pool(name="flip", bufs=CHUNKS) as flip,
-        tc.psum_pool(name="prod", bufs=4) as prod,
+        tc.tile_pool(name="done", bufs=PIECES * HALVES) as done,
     ):
+        gain_row = held.tile([1, D], F32, name="gain_row")
+        nc.sync.dma_start(gain_row[:], att_scale.rearrange("d one -> one d"))
+        table_chunks = table.rearrange("(c k p) d -> c p k d", k=BLOCKS_PER_CHUNK, p=P)
         rows = [held.tile([P, BLOCKS_PER_CHUNK, D], BF16, name=f"rows{c}") for c in range(CHUNKS)]
         for c in range(CHUNKS):
             nc.sync.dma_start(rows[c][:], table_chunks[c])
         offsets = held.tile([P, N // 16], U16, name="offsets")
         nc.sync.dma_start(offsets[:], offs)
-        gain = held.tile([D, 1], F32, name="gain")
-        nc.scalar.dma_start(gain[:], att_scale)
         weights = held.tile([D, M], BF16, name="weights")
-        nc.scalar.dma_start(weights[:], w)
-        bias = [held.tile([P, 1], F32, name=f"bias{h}") for h in range(M // P)]
-        for h in range(M // P):
-            nc.scalar.dma_start(bias[h][:], b[h * P : (h + 1) * P, :])
+        nc.sync.dma_start(weights[:], w)
+        bias = [held.tile([P, 1], F32, name=f"bias{h}") for h in range(HALVES)]
+        for h in range(HALVES):
+            nc.sync.dma_start(bias[h][:], b[h * P : (h + 1) * P, :])
 
-        identity = held.tile([P, P], F32, name="identity")
+        identity = held.tile([P, P], BF16, name="identity")
         make_identity(nc, identity[:])
         eps = held.tile([P, 1], F32, name="eps")
         nc.vector.memset(eps[:], EPS)
+        ones = held.tile([1, P], F32, name="ones")
+        nc.vector.memset(ones[:], 1.0)
         first = held.tile([P, 1], F32, name="first")
         nc.scalar.activation(first[:], eps[:], ACT.Sqrt)
 
-        normed = held.tile([D, V], BF16, name="normed")
+        rstd = [held.tile([P, BLOCKS_PER_CHUNK], F32, name=f"rstd{c}") for c in range(CHUNKS)]
         for c in range(CHUNKS):
             sumsq = work.tile([P, BLOCKS_PER_CHUNK], F32, name="sumsq")
             for k in range(BLOCKS_PER_CHUNK):
@@ -55,31 +58,43 @@ def tile_gqa_kernel(tc, table, att_scale, w, b, offs, out):
                 )
             rms = work.tile([P, BLOCKS_PER_CHUNK], F32, name="rms")
             nc.scalar.activation(rms[:], sumsq[:], ACT.Sqrt, bias=eps[:], scale=1.0 / D)
-            rstd = work.tile([P, BLOCKS_PER_CHUNK], F32, name="rstd")
-            nc.vector.reciprocal(rstd[:], rms[:])
-            scaled = work.tile([P, BLOCKS_PER_CHUNK, D], F32, name="scaled")
-            for k in range(BLOCKS_PER_CHUNK):
-                nc.vector.tensor_scalar_mul(scaled[:, k, :], rows[c][:, k, :], rstd[:, k : k + 1])
-            flipped = flip.tile([D, CHUNK], F32, name="flipped")
-            for k in range(BLOCKS_PER_CHUNK):
-                nc.tensor.transpose(flipped[:, k * P : (k + 1) * P], scaled[:, k, :], identity[:])
-            nc.vector.tensor_scalar_mul(
-                normed[:, c * CHUNK : (c + 1) * CHUNK].rearrange("d (p k) -> d p k", k=BLOCKS_PER_CHUNK),
-                flipped[:].rearrange("d (k p) -> d p k", k=BLOCKS_PER_CHUNK),
-                gain[:],
-            )
+            nc.vector.reciprocal(rstd[c][:], rms[:])
 
-        for j in range(N // PIECE):
-            looked_up = normed[:].indirect(offsets[:, j * (PIECE // 16) : (j + 1) * (PIECE // 16)])
-            for h in range(M // P):
-                product = prod.tile([P, PIECE], F32, name="product")
-                nc.tensor.matmul(
-                    product[:], weights[:, h * P : (h + 1) * P], looked_up, start=True, stop=True
-                )
-                biased = done.tile([P, PIECE], F32, name="biased")
-                if h == 0:
-                    nc.scalar.activation(biased[:], product[:], ACT.Identity, bias=bias[h][:])
-                    nc.scalar.dma_start(out[h * P : (h + 1) * P, j * PIECE : (j + 1) * PIECE], biased[:])
+        normed = held.tile([D, V], BF16, name="normed")
+        with (
+            tc.psum_pool(name="spread", bufs=1) as spread,
+            tc.psum_pool(name="flip", bufs=CHUNKS) as flip,
+        ):
+            gain = spread.tile([P, D], F32, name="gain")
+            nc.tensor.matmul(gain[:], ones[:], gain_row[:], start=True, stop=True)
+            for c in range(CHUNKS):
+                normed_rows = work.tile([P, BLOCKS_PER_CHUNK, D], BF16, name="normed_rows")
+                flipped = flip.tile([D, CHUNK], BF16, name="flipped")
+                for k in range(BLOCKS_PER_CHUNK):
+                    nc.vector.scalar_tensor_tensor(
+                        normed_rows[:, k, :], rows[c][:, k, :], rstd[c][:, k : k + 1], gain[:], MULT, MULT
+                    )
+                    nc.tensor.transpose(
+                        flipped[:, k * P : (k + 1) * P], normed_rows[:, k, :], identity[:]
+                    )
+                if c < CHUNKS - 1:
+                    nc.scalar.copy(normed[:, c * CHUNK : (c + 1) * CHUNK], flipped[:])
                 else:
-                    nc.vector.tensor_scalar_add(biased[:], product[:], bias[h][:])
-                    nc.sync.dma_start(out[h * P : (h + 1) * P, j * PIECE : (j + 1) * PIECE], biased[:])
+                    nc.vector.tensor_copy(normed[:, c * CHUNK : (c + 1) * CHUNK], flipped[:])
+
+        with tc.psum_pool(name="prod", bufs=PIECES * HALVES) as prod:
+            for j in range(PIECES):
+                looked_up = normed[:].indirect(offsets[:, j * (PIECE // 16) : (j + 1) * (PIECE // 16)])
+                for h in range(HALVES):
+                    product = prod.tile([P, PIECE], F32, name="product")
+                    nc.tensor.matmul(
+                        product[:], weights[:, h * P : (h + 1) * P], looked_up, start=True, stop=True
+                    )
+                    biased = done.tile([P, PIECE], F32, name="biased")
+                    out_part = out[h * P : (h + 1) * P, j * PIECE : (j + 1) * PIECE]
+                    if h == 0:
+                        nc.scalar.activation(biased[:], product[:], ACT.Identity, bias=bias[h][:])
+                        nc.scalar.dma_start(out_part, biased[:])
+                    else:
+                        nc.vector.tensor_scalar_add(biased[:], product[:], bias[h][:])
+                        nc.sync.dma_start(out_part, biased[:])

@@ -49,15 +49,23 @@ def tile_gqa_kernel(tc, table, att_scale, w, b, offs, out):
         nc.scalar.activation(first[:], eps[:], ACT.Sqrt)
 
         rstd = [held.tile([P, BLOCKS_PER_CHUNK], F32, name=f"rstd{c}") for c in range(CHUNKS)]
+        last = BLOCKS_PER_CHUNK - 1
         for c in range(CHUNKS):
-            sumsq = work.tile([P, BLOCKS_PER_CHUNK], F32, name="sumsq")
-            for k in range(BLOCKS_PER_CHUNK):
-                squares = work.tile([P, D], BF16, name="squares")
+            sumsq_scalar = work.tile([P, last], F32, name="sumsq_scalar")
+            for k in range(last):
+                squares_scalar = work.tile([P, D], BF16, name="squares_scalar")
                 nc.scalar.activation(
-                    squares[:], rows[c][:, k, :], ACT.Square, accum_out=sumsq[:, k : k + 1]
+                    squares_scalar[:], rows[c][:, k, :], ACT.Square, accum_out=sumsq_scalar[:, k : k + 1]
                 )
+            sumsq_vector = work.tile([P, 1], F32, name="sumsq_vector")
+            squares_vector = work.tile([P, D], BF16, name="squares_vector")
+            nc.vector.scalar_tensor_tensor(
+                squares_vector[:], rows[c][:, last, :], 1.0, rows[c][:, last, :], MULT, MULT,
+                accum_out=sumsq_vector[:],
+            )
             rms = work.tile([P, BLOCKS_PER_CHUNK], F32, name="rms")
-            nc.scalar.activation(rms[:], sumsq[:], ACT.Sqrt, bias=eps[:], scale=1.0 / D)
+            nc.scalar.activation(rms[:, 0:last], sumsq_scalar[:], ACT.Sqrt, bias=eps[:], scale=1.0 / D)
+            nc.scalar.activation(rms[:, last:], sumsq_vector[:], ACT.Sqrt, bias=eps[:], scale=1.0 / D)
             nc.vector.reciprocal(rstd[c][:], rms[:])
 
         normed = held.tile([D, V], BF16, name="normed")

@@ -46,27 +46,23 @@ def tile_gqa_kernel(tc, table, att_scale, w, b, offs, out):
         ones = held.tile([1, P], F32, name="ones")
         nc.vector.memset(ones[:], 1.0)
         first = held.tile([P, 1], F32, name="first")
-        nc.scalar.activation(first[:], eps[:], ACT.Sqrt)
+        nc.scalar.activation(first[:], eps[:], ACT.Abs_reciprocal_sqrt)
 
         rstd = [held.tile([P, BLOCKS_PER_CHUNK], F32, name=f"rstd{c}") for c in range(CHUNKS)]
         last = BLOCKS_PER_CHUNK - 1
         for c in range(CHUNKS):
-            sumsq_scalar = work.tile([P, last], F32, name="sumsq_scalar")
+            sumsq = work.tile([P, BLOCKS_PER_CHUNK], F32, name="sumsq")
             for k in range(last):
                 squares_scalar = work.tile([P, D], BF16, name="squares_scalar")
                 nc.scalar.activation(
-                    squares_scalar[:], rows[c][:, k, :], ACT.Square, accum_out=sumsq_scalar[:, k : k + 1]
+                    squares_scalar[:], rows[c][:, k, :], ACT.Square, accum_out=sumsq[:, k : k + 1]
                 )
-            sumsq_vector = work.tile([P, 1], F32, name="sumsq_vector")
             squares_vector = work.tile([P, D], BF16, name="squares_vector")
             nc.vector.scalar_tensor_tensor(
                 squares_vector[:], rows[c][:, last, :], 1.0, rows[c][:, last, :], MULT, MULT,
-                accum_out=sumsq_vector[:],
+                accum_out=sumsq[:, last:],
             )
-            rms = work.tile([P, BLOCKS_PER_CHUNK], F32, name="rms")
-            nc.scalar.activation(rms[:, 0:last], sumsq_scalar[:], ACT.Sqrt, bias=eps[:], scale=1.0 / D)
-            nc.scalar.activation(rms[:, last:], sumsq_vector[:], ACT.Sqrt, bias=eps[:], scale=1.0 / D)
-            nc.vector.reciprocal(rstd[c][:], rms[:])
+            nc.scalar.activation(rstd[c][:], sumsq[:], ACT.Abs_reciprocal_sqrt, bias=eps[:], scale=1.0 / D)
 
         normed = held.tile([D, V], BF16, name="normed")
         with (

@@ -25,12 +25,12 @@ def tile_gqa_kernel(tc, table, att_scale, w, b, offs, out):
         tc.tile_pool(name="work", bufs=2) as work,
         tc.tile_pool(name="done", bufs=PIECES * HALVES) as done,
     ):
-        gain_row = held.tile([1, D], F32, name="gain_row")
-        nc.sync.dma_start(gain_row[:], att_scale.rearrange("d one -> one d"))
         table_chunks = table.rearrange("(c k p) d -> c p k d", k=BLOCKS_PER_CHUNK, p=P)
         rows = [held.tile([P, BLOCKS_PER_CHUNK, D], BF16, name=f"rows{c}") for c in range(CHUNKS)]
         for c in range(CHUNKS):
             nc.sync.dma_start(rows[c][:], table_chunks[c])
+        gain = held.tile([D, 1], F32, name="gain")
+        nc.sync.dma_start(gain[:], att_scale)
         offsets = held.tile([P, N // 16], U16, name="offsets")
         nc.sync.dma_start(offsets[:], offs)
         weights = held.tile([D, M], BF16, name="weights")
@@ -39,52 +39,44 @@ def tile_gqa_kernel(tc, table, att_scale, w, b, offs, out):
         for h in range(HALVES):
             nc.sync.dma_start(bias[h][:], b[h * P : (h + 1) * P, :])
 
-        identity = held.tile([P, P], BF16, name="identity")
+        identity = held.tile([P, P], F32, name="identity")
         make_identity(nc, identity[:])
         eps = held.tile([P, 1], F32, name="eps")
         nc.vector.memset(eps[:], EPS)
-        ones = held.tile([1, P], F32, name="ones")
-        nc.vector.memset(ones[:], 1.0)
         first = held.tile([P, 1], F32, name="first")
         nc.scalar.activation(first[:], eps[:], ACT.Abs_reciprocal_sqrt)
 
         rstd = [held.tile([P, BLOCKS_PER_CHUNK], F32, name=f"rstd{c}") for c in range(CHUNKS)]
-        last = BLOCKS_PER_CHUNK - 1
         for c in range(CHUNKS):
             sumsq = work.tile([P, BLOCKS_PER_CHUNK], F32, name="sumsq")
-            for k in range(last):
-                squares_scalar = work.tile([P, D], BF16, name="squares_scalar")
-                nc.scalar.activation(
-                    squares_scalar[:], rows[c][:, k, :], ACT.Square, accum_out=sumsq[:, k : k + 1]
-                )
-            squares_vector = work.tile([P, D], BF16, name="squares_vector")
-            nc.vector.scalar_tensor_tensor(
-                squares_vector[:], rows[c][:, last, :], 1.0, rows[c][:, last, :], MULT, MULT,
-                accum_out=sumsq[:, last:],
-            )
+            for k in range(BLOCKS_PER_CHUNK):
+                if k % 2 == 0:
+                    squares_scalar = work.tile([P, D], BF16, name="squares_scalar")
+                    nc.scalar.activation(
+                        squares_scalar[:], rows[c][:, k, :], ACT.Square, accum_out=sumsq[:, k : k + 1]
+                    )
+                else:
+                    squares_vector = work.tile([P, D], BF16, name="squares_vector")
+                    nc.vector.scalar_tensor_tensor(
+                        squares_vector[:], rows[c][:, k, :], 1.0, rows[c][:, k, :], MULT, MULT,
+                        accum_out=sumsq[:, k : k + 1],
+                    )
             nc.scalar.activation(rstd[c][:], sumsq[:], ACT.Abs_reciprocal_sqrt, bias=eps[:], scale=1.0 / D)
 
         normed = held.tile([D, V], BF16, name="normed")
-        with (
-            tc.psum_pool(name="spread", bufs=1) as spread,
-            tc.psum_pool(name="flip", bufs=CHUNKS) as flip,
-        ):
-            gain = spread.tile([P, D], F32, name="gain")
-            nc.tensor.matmul(gain[:], ones[:], gain_row[:], start=True, stop=True)
+        with tc.psum_pool(name="flip", bufs=CHUNKS) as flip:
             for c in range(CHUNKS):
-                normed_rows = work.tile([P, BLOCKS_PER_CHUNK, D], BF16, name="normed_rows")
-                flipped = flip.tile([D, CHUNK], BF16, name="flipped")
+                scaled_rows = work.tile([P, BLOCKS_PER_CHUNK, D], F32, name="scaled_rows")
+                flipped = flip.tile([D, CHUNK], F32, name="flipped")
                 for k in range(BLOCKS_PER_CHUNK):
-                    nc.vector.scalar_tensor_tensor(
-                        normed_rows[:, k, :], rows[c][:, k, :], rstd[c][:, k : k + 1], gain[:], MULT, MULT
-                    )
+                    nc.vector.tensor_scalar_mul(scaled_rows[:, k, :], rows[c][:, k, :], rstd[c][:, k : k + 1])
                     nc.tensor.transpose(
-                        flipped[:, k * P : (k + 1) * P], normed_rows[:, k, :], identity[:]
+                        flipped[:, k * P : (k + 1) * P], scaled_rows[:, k, :], identity[:]
                     )
                 if c < CHUNKS - 1:
-                    nc.scalar.copy(normed[:, c * CHUNK : (c + 1) * CHUNK], flipped[:])
+                    nc.scalar.activation(normed[:, c * CHUNK : (c + 1) * CHUNK], flipped[:], ACT.Copy, scale=gain[:])
                 else:
-                    nc.vector.tensor_copy(normed[:, c * CHUNK : (c + 1) * CHUNK], flipped[:])
+                    nc.vector.tensor_scalar_mul(normed[:, c * CHUNK : (c + 1) * CHUNK], flipped[:], gain[:])
 
         with tc.psum_pool(name="prod", bufs=PIECES * HALVES) as prod:
             for j in range(PIECES):

import concourse.mybir as mybir
from concourse.masks import make_identity

BF16, F32, U16 = mybir.dt.bfloat16, mybir.dt.float32, mybir.dt.uint16
ACT = mybir.ActivationFunctionType
MULT = mybir.AluOpType.mult

P = 128
V, D, M, N = 2048, 128, 256, 1024
EPS = 1e-5
BLOCKS_PER_CHUNK = 4
CHUNK = BLOCKS_PER_CHUNK * P
CHUNKS = V // CHUNK
PIECE = 256
PIECES = N // PIECE
HALVES = M // P
FLOPS = 2 * D * M * N


def tile_gqa_kernel(tc, table, att_scale, w, b, offs, out):
    nc = tc.nc

    with (
        tc.tile_pool(name="held", bufs=1) as held,
        tc.tile_pool(name="work", bufs=2) as work,
        tc.tile_pool(name="done", bufs=PIECES * HALVES) as done,
    ):
        table_chunks = table.rearrange("(c k p) d -> c p k d", k=BLOCKS_PER_CHUNK, p=P)
        rows = [held.tile([P, BLOCKS_PER_CHUNK, D], BF16, name=f"rows{c}") for c in range(CHUNKS)]
        for c in range(CHUNKS):
            nc.sync.dma_start(rows[c][:], table_chunks[c])
        gain = held.tile([D, 1], F32, name="gain")
        nc.sync.dma_start(gain[:], att_scale)
        offsets = held.tile([P, N // 16], U16, name="offsets")
        nc.sync.dma_start(offsets[:], offs)
        weights = held.tile([D, M], BF16, name="weights")
        nc.sync.dma_start(weights[:], w)
        bias = [held.tile([P, 1], F32, name=f"bias{h}") for h in range(HALVES)]
        for h in range(HALVES):
            nc.sync.dma_start(bias[h][:], b[h * P : (h + 1) * P, :])

        identity = held.tile([P, P], F32, name="identity")
        make_identity(nc, identity[:])
        eps = held.tile([P, 1], F32, name="eps")
        nc.vector.memset(eps[:], EPS)
        first = held.tile([P, 1], F32, name="first")
        nc.scalar.activation(first[:], eps[:], ACT.Abs_reciprocal_sqrt)

        rstd = [held.tile([P, BLOCKS_PER_CHUNK], F32, name=f"rstd{c}") for c in range(CHUNKS)]
        for c in range(CHUNKS):
            sumsq = work.tile([P, BLOCKS_PER_CHUNK], F32, name="sumsq")
            for k in range(BLOCKS_PER_CHUNK):
                if k % 2 == 0:
                    squares_scalar = work.tile([P, D], BF16, name="squares_scalar")
                    nc.scalar.activation(
                        squares_scalar[:], rows[c][:, k, :], ACT.Square, accum_out=sumsq[:, k : k + 1]
                    )
                else:
                    squares_vector = work.tile([P, D], BF16, name="squares_vector")
                    nc.vector.scalar_tensor_tensor(
                        squares_vector[:], rows[c][:, k, :], 1.0, rows[c][:, k, :], MULT, MULT,
                        accum_out=sumsq[:, k : k + 1],
                    )
            nc.scalar.activation(rstd[c][:], sumsq[:], ACT.Abs_reciprocal_sqrt, bias=eps[:], scale=1.0 / D)

        normed = held.tile([D, V], BF16, name="normed")
        with tc.psum_pool(name="flip", bufs=CHUNKS) as flip:
            for c in range(CHUNKS):
                scaled_rows = work.tile([P, BLOCKS_PER_CHUNK, D], F32, name="scaled_rows")
                flipped = flip.tile([D, CHUNK], F32, name="flipped")
                for k in range(BLOCKS_PER_CHUNK):
                    nc.vector.tensor_scalar_mul(scaled_rows[:, k, :], rows[c][:, k, :], rstd[c][:, k : k + 1])
                    nc.tensor.transpose(
                        flipped[:, k * P : (k + 1) * P], scaled_rows[:, k, :], identity[:]
                    )
                if c < CHUNKS - 1:
                    nc.scalar.activation(normed[:, c * CHUNK : (c + 1) * CHUNK], flipped[:], ACT.Copy, scale=gain[:])
                else:
                    nc.vector.tensor_scalar_mul(normed[:, c * CHUNK : (c + 1) * CHUNK], flipped[:], gain[:])

        with tc.psum_pool(name="prod", bufs=PIECES * HALVES) as prod:
            for j in range(PIECES):
                looked_up = normed[:].indirect(offsets[:, j * (PIECE // 16) : (j + 1) * (PIECE // 16)])
                for h in range(HALVES):
                    product = prod.tile([P, PIECE], F32, name="product")
                    nc.tensor.matmul(
                        product[:], weights[:, h * P : (h + 1) * P], looked_up, start=True, stop=True
                    )
                    biased = done.tile([P, PIECE], F32, name="biased")
                    out_part = out[h * P : (h + 1) * P, j * PIECE : (j + 1) * PIECE]
                    if h == 0:
                        nc.scalar.activation(biased[:], product[:], ACT.Identity, bias=bias[h][:])
                        nc.scalar.dma_start(out_part, biased[:])
                    else:
                        nc.vector.tensor_scalar_add(biased[:], product[:], bias[h][:])
                        nc.sync.dma_start(out_part, biased[:])
